import numpy as np
import ml_dtypes


def mxq(x, axis, fmt="e4m3"):
    dtype, down = {"e4m3": (ml_dtypes.float8_e4m3fn, 7), "e5m2": (ml_dtypes.float8_e5m2, 14)}[fmt]
    v = np.moveaxis(np.asarray(x, np.float32).astype(ml_dtypes.bfloat16).astype(np.float64), axis, -1)
    blocks = v.reshape(v.shape[:-1] + (-1, 32))
    amax = np.abs(blocks).max(-1, keepdims=True)
    byte = np.maximum(np.where(amax > 0, np.frexp(amax)[1] - 1 + 127, 0) - down, 1)
    scale = np.exp2(byte - 127.0)
    codes = (blocks / scale).astype(np.float32).astype(dtype).astype(np.float64)
    return np.moveaxis((codes * scale).reshape(v.shape), -1, axis)


WIDE = False


def mx_kscale(k):
    if not WIDE:
        return np.ones(k)
    levels = np.array([20, -20, 10, -10, 0])
    a = np.random.permutation(np.resize(levels, k // 512 * 4)).reshape(k // 512, 4)
    idx = np.arange(k)
    return np.exp2(a[idx // 512, idx % 128 // 32])


BF16 = ml_dtypes.bfloat16


def bf(x):
    return np.asarray(x, np.float32).astype(BF16)


def f64(x):
    return np.asarray(x).astype(np.float64)


B, I, H = 4096, 512, 512
DT = 0.1


def sigmoid(v):
    return 1.0 / (1.0 + np.exp(-v))


def setup_inputs():
    s = mx_kscale(B)[:, None]
    wt = bf(np.random.standard_normal((H, I + H)) * 1.5 / np.sqrt(I + H))
    x0 = bf(np.random.standard_normal((B, I)))
    h0 = bf(np.random.standard_normal((B, H)))
    W_rec = bf(np.random.standard_normal((H, H)) * 1.0 / np.sqrt(H))
    W_in_w = bf(np.random.standard_normal((H, I)) * 0.8 / np.sqrt(I))
    W_in_b = bf(np.random.standard_normal(H) * 0.5)
    tau_base = bf(0.3 + 0.3 * np.random.random(H))
    tau_adapt_b = bf(np.random.standard_normal(H) * 0.5)
    g = bf(np.random.standard_normal((B, H)) * np.exp2(np.random.randint(-12, 1, (B, 1))) * 4.0 / s)
    tau_logits = f64(x0) @ f64(wt)[:, :I].T + f64(h0) @ f64(wt)[:, I:].T + f64(tau_adapt_b)
    drive = np.tanh(f64(h0) @ f64(W_rec).T + f64(x0) @ f64(W_in_w).T + f64(W_in_b)) - f64(h0)
    return {"x": bf(f64(x0) * s),
            "hidden": bf(f64(h0) * s),
            "W_rec": W_rec,
            "W_in_w": W_in_w,
            "W_in_b": W_in_b,
            "tau_base": tau_base,
            "tau_adapt_w": wt,
            "tau_adapt_b": tau_adapt_b,
            "tau_logits": np.asarray(tau_logits, np.float32),
            "drive": np.asarray(drive, np.float32),
            "grad_out": g}


def reference(x, hidden, W_rec, W_in_w, W_in_b, tau_base, tau_adapt_w, tau_adapt_b, tau_logits, drive, grad_out):
    sg = sigmoid(f64(tau_logits))
    dl = -DT * f64(grad_out) * f64(drive) * sg * (1.0 - sg) / (f64(tau_base) * (0.5 + sg) ** 2)
    dlq = mxq(dl, 0, "e5m2")
    gx = dlq.T @ mxq(f64(x), 0, "e4m3")
    gh = dlq.T @ mxq(f64(hidden), 0, "e4m3")
    return np.concatenate([gx, gh], axis=1)

@@ -1,0 +1,186 @@
+import math
+from contextlib import ExitStack
+
+import concourse.mybir as mybir
+from concourse.masks import make_identity
+
+F32 = mybir.dt.float32
+BF16 = mybir.dt.bfloat16
+U32 = mybir.dt.uint32
+U8 = mybir.dt.uint8
+E4M3_X4 = mybir.dt.float8_e4m3fn_x4
+E5M2_X4 = mybir.dt.float8_e5m2_x4
+ACT = mybir.ActivationFunctionType
+ALU = mybir.AluOpType
+
+P = 128
+PACK = 4
+K_PASS = P * PACK
+TOKENS = 4096
+WIDTH = 512
+CHUNKS = TOKENS // K_PASS
+M_TILES = WIDTH // P
+RUN = 4
+
+LOAD_BUFS = 4
+VECTOR_REGROUP_CHUNKS = 1
+
+HALF_LN3 = 0.5 * math.log(3.0)
+
+FLOPS = 2 * TOKENS * WIDTH * (2 * WIDTH)
+BYTES = 3 * TOKENS * WIDTH * 2 + 2 * TOKENS * WIDTH * 4 + WIDTH * 2 + WIDTH * 2 * WIDTH * 4
+
+
+def chunk_rows(tensor, i):
+    return tensor[i * K_PASS : (i + 1) * K_PASS, :].rearrange("(p t) w -> p t w", t=PACK)
+
+
+def by_token(tile_ap):
+    return tile_ap.rearrange("p t (c i) -> p c t i", i=RUN)
+
+
+def by_column(tile_ap):
+    return tile_ap.rearrange("p (c i) t -> p c t i", i=RUN)
+
+
+def tile_liquidcell_pa_t_v_kernel(
+    tc,
+    x,
+    hidden,
+    W_rec,
+    W_in_w,
+    W_in_b,
+    tau_base,
+    tau_adapt_w,
+    tau_adapt_b,
+    tau_logits,
+    drive,
+    grad_out,
+    out,
+):
+    nc = tc.nc
+    with ExitStack() as ctx:
+        const = ctx.enter_context(tc.tile_pool(name="const", bufs=1))
+        loads = ctx.enter_context(tc.tile_pool(name="loads", bufs=LOAD_BUFS))
+        grouped = ctx.enter_context(tc.tile_pool(name="grouped", bufs=3))
+        quant = ctx.enter_context(tc.tile_pool(name="quant", bufs=3))
+        results = ctx.enter_context(tc.tile_pool(name="results", bufs=M_TILES))
+        psum = ctx.enter_context(tc.psum_pool(name="psum", bufs=1))
+        ctx.enter_context(tc.manual_schedule())
+
+        raw = {}
+        ready = {}
+        packed = {}
+
+        def load(i):
+            logit = loads.tile([P, PACK, WIDTH], F32, name="logit")
+            nc.sync.dma_start(out=logit[:], in_=chunk_rows(tau_logits, i))
+            x_raw = loads.tile([P, PACK, WIDTH], BF16, name="x_raw")
+            nc.sync.dma_start(out=x_raw[:], in_=chunk_rows(x, i))
+            h_raw = loads.tile([P, PACK, WIDTH], BF16, name="h_raw")
+            nc.sync.dma_start(out=h_raw[:], in_=chunk_rows(hidden, i))
+            grad = loads.tile([P, PACK, WIDTH], BF16, name="grad")
+            nc.sync.dma_start(out=grad[:], in_=chunk_rows(grad_out, i))
+            product = loads.tile([P, PACK, WIDTH], F32, name="product")
+            nc.sync.dma_start(out=product[:], in_=chunk_rows(drive, i))
+            raw[i] = {"logit": logit, "x": x_raw, "grad": grad, "product": product, "h": h_raw}
+
+        def regroup(copy, i, operand):
+            tile = grouped.tile([P, WIDTH, PACK], BF16, name="ready_" + operand, align_bytes=64)
+            copy(out=by_column(tile[:]), in_=by_token(raw[i][operand][:]))
+            ready[(i, operand)] = tile
+
+        def quantise(i, operand, fmt):
+            codes = quant.tile([P, WIDTH], U32, name="codes_" + operand, align_bytes=64)
+            scales = quant.tile([P, WIDTH], U8, name="scales_" + operand, align_bytes=64)
+            nc.vector.quantize_mx(
+                out=codes[:].bitcast(fmt),
+                scales=scales[:],
+                in_=ready[(i, operand)][:].rearrange("p w t -> p (w t)"),
+            )
+            packed[(i, operand)] = (codes, scales)
+
+        tau_col = const.tile([P, PACK], BF16, name="tau_col")
+        nc.sync.dma_start(out=tau_col[:], in_=tau_base.rearrange("(p a) -> p a", a=PACK))
+        for i in range(LOAD_BUFS):
+            load(i)
+        identity = const.tile([P, P], F32, name="identity")
+        make_identity(nc, identity[:])
+        tau30 = const.tile([P, PACK], F32, name="tau30")
+        nc.vector.tensor_scalar(out=tau30[:], in0=tau_col[:], scalar1=30.0, scalar2=None, op0=ALU.mult)
+        gain_col = const.tile([P, PACK], F32, name="gain_col")
+        nc.vector.reciprocal(out=gain_col[:], in_=tau30[:])
+        gain_psum = psum.tile([P, PACK, P], F32, name="gain_psum", tag="acc_3_1")
+        for a in range(PACK):
+            nc.tensor.matmul(
+                out=gain_psum[:, a, :],
+                lhsT=gain_col[:, a : a + 1].to_broadcast([P, P]),
+                rhs=identity[:],
+                start=True,
+                stop=True,
+            )
+        gain = const.tile([P, WIDTH], F32, name="gain")
+        nc.vector.tensor_copy(
+            out=gain[:].rearrange("p (n a) -> p n a", a=PACK),
+            in_=gain_psum[:].rearrange("p a n -> p n a"),
+        )
+        gain_by_token = (
+            gain[:].rearrange("p (c i) -> p c i", i=RUN).unsqueeze(2).to_broadcast([P, WIDTH // RUN, PACK, RUN])
+        )
+
+        acc = {}
+        for m in range(M_TILES):
+            for half in range(2):
+                acc[(m, half)] = psum.tile([P, WIDTH], F32, name="acc_%d_%d" % (m, half))
+
+        def multiply(i):
+            dl_codes, dl_scales = packed[(i, "dl")]
+            for m in range(M_TILES):
+                rows = slice(m * P, (m + 1) * P)
+                for half, operand in enumerate(("x", "h")):
+                    codes, scales = packed[(i, operand)]
+                    nc.tensor.matmul_mx(
+                        out=acc[(m, half)][:],
+                        lhsT=dl_codes[:, rows].bitcast(E5M2_X4),
+                        lhsT_scale=dl_scales[:, rows],
+                        rhs=codes[:].bitcast(E4M3_X4),
+                        rhs_scale=scales[:],
+                        start=(i == 0),
+                        stop=(i == CHUNKS - 1),
+                    )
+
+        for i in range(CHUNKS):
+            logit = raw[i]["logit"][:].rearrange("p t w -> p (t w)")
+            product = raw[i]["product"][:].rearrange("p t w -> p (t w)")
+            grad = raw[i]["grad"][:].rearrange("p t w -> p (t w)")
+            copy = nc.vector.tensor_copy if i < VECTOR_REGROUP_CHUNKS else nc.scalar.copy
+
+            nc.scalar.activation(out=logit, in_=logit, func=ACT.Tanh, bias=HALF_LN3, scale=0.5)
+            regroup(copy, i, "x")
+            nc.scalar.activation(out=logit, in_=logit, func=ACT.Square)
+            regroup(copy, i, "h")
+
+            nc.vector.tensor_tensor(out=product, in0=grad, in1=product, op=ALU.mult)
+            if i > 0:
+                quantise(i - 1, "dl", E5M2_X4)
+                multiply(i - 1)
+            quantise(i, "x", E4M3_X4)
+            nc.vector.scalar_tensor_tensor(
+                out=product, in0=logit, scalar=1.0, in1=product, op0=ALU.subtract, op1=ALU.mult
+            )
+            quantise(i, "h", E4M3_X4)
+            dl_ready = grouped.tile([P, WIDTH, PACK], BF16, name="ready_dl", align_bytes=64)
+            nc.vector.tensor_tensor(
+                out=by_column(dl_ready[:]), in0=by_token(raw[i]["product"][:]), in1=gain_by_token, op=ALU.mult
+            )
+            ready[(i, "dl")] = dl_ready
+            if i + LOAD_BUFS < CHUNKS:
+                load(i + LOAD_BUFS)
+        quantise(CHUNKS - 1, "dl", E5M2_X4)
+        multiply(CHUNKS - 1)
+
+        for m in range(M_TILES):
+            result = results.tile([P, 2 * WIDTH], F32, name="result")
+            nc.scalar.copy(out=result[:, :WIDTH], in_=acc[(m, 0)][:])
+            nc.vector.tensor_copy(out=result[:, WIDTH:], in_=acc[(m, 1)][:])
+            nc.sync.dma_start(out=out[m * P : (m + 1) * P, :], in_=result[:])

@@ -23,7 +23,8 @@ M_TILES = WIDTH // P
 RUN = 4
 
 LOAD_BUFS = 4
-VECTOR_REGROUP_CHUNKS = 1
+FIRST_CHUNK_PIECES = 2
+VECTOR_SHARE = 4
 
 HALF_LN3 = 0.5 * math.log(3.0)
 
@@ -33,6 +34,12 @@ BYTES = 3 * TOKENS * WIDTH * 2 + 2 * TOKENS * WIDTH * 4 + WIDTH * 2 + WIDTH * 2 
 
 def chunk_rows(tensor, i):
     return tensor[i * K_PASS : (i + 1) * K_PASS, :].rearrange("(p t) w -> p t w", t=PACK)
+
+
+def token_pieces(i):
+    pieces = FIRST_CHUNK_PIECES if i == 0 else 1
+    tokens = PACK // pieces
+    return [slice(k * tokens, (k + 1) * tokens) for k in range(pieces)]
 
 
 def by_token(tile_ap):
@@ -64,7 +71,7 @@ def tile_liquidcell_pa_t_v_kernel(
         loads = ctx.enter_context(tc.tile_pool(name="loads", bufs=LOAD_BUFS))
         grouped = ctx.enter_context(tc.tile_pool(name="grouped", bufs=3))
         quant = ctx.enter_context(tc.tile_pool(name="quant", bufs=3))
-        results = ctx.enter_context(tc.tile_pool(name="results", bufs=M_TILES))
+        results = ctx.enter_context(tc.tile_pool(name="results", bufs=2 * M_TILES))
         psum = ctx.enter_context(tc.psum_pool(name="psum", bufs=1))
         ctx.enter_context(tc.manual_schedule())
 
@@ -72,22 +79,29 @@ def tile_liquidcell_pa_t_v_kernel(
         ready = {}
         packed = {}
 
-        def load(i):
+        def load_factors(i):
             logit = loads.tile([P, PACK, WIDTH], F32, name="logit")
-            nc.sync.dma_start(out=logit[:], in_=chunk_rows(tau_logits, i))
+            grad = loads.tile([P, PACK, WIDTH], BF16, name="grad")
+            product = loads.tile([P, PACK, WIDTH], F32, name="product")
+            for tokens in token_pieces(i):
+                nc.sync.dma_start(out=logit[:, tokens, :], in_=chunk_rows(tau_logits, i)[:, tokens, :])
+                nc.sync.dma_start(out=grad[:, tokens, :], in_=chunk_rows(grad_out, i)[:, tokens, :])
+                nc.sync.dma_start(out=product[:, tokens, :], in_=chunk_rows(drive, i)[:, tokens, :])
+            raw[(i, "logit")] = logit
+            raw[(i, "grad")] = grad
+            raw[(i, "product")] = product
+
+        def load_operands(i):
             x_raw = loads.tile([P, PACK, WIDTH], BF16, name="x_raw")
             nc.sync.dma_start(out=x_raw[:], in_=chunk_rows(x, i))
             h_raw = loads.tile([P, PACK, WIDTH], BF16, name="h_raw")
             nc.sync.dma_start(out=h_raw[:], in_=chunk_rows(hidden, i))
-            grad = loads.tile([P, PACK, WIDTH], BF16, name="grad")
-            nc.sync.dma_start(out=grad[:], in_=chunk_rows(grad_out, i))
-            product = loads.tile([P, PACK, WIDTH], F32, name="product")
-            nc.sync.dma_start(out=product[:], in_=chunk_rows(drive, i))
-            raw[i] = {"logit": logit, "x": x_raw, "grad": grad, "product": product, "h": h_raw}
+            raw[(i, "x")] = x_raw
+            raw[(i, "h")] = h_raw
 
         def regroup(copy, i, operand):
             tile = grouped.tile([P, WIDTH, PACK], BF16, name="ready_" + operand, align_bytes=64)
-            copy(out=by_column(tile[:]), in_=by_token(raw[i][operand][:]))
+            copy(out=by_column(tile[:]), in_=by_token(raw[(i, operand)][:]))
             ready[(i, operand)] = tile
 
         def quantise(i, operand, fmt):
@@ -102,8 +116,11 @@ def tile_liquidcell_pa_t_v_kernel(
 
         tau_col = const.tile([P, PACK], BF16, name="tau_col")
         nc.sync.dma_start(out=tau_col[:], in_=tau_base.rearrange("(p a) -> p a", a=PACK))
-        for i in range(LOAD_BUFS):
-            load(i)
+        load_factors(0)
+        for i in range(1, LOAD_BUFS):
+            load_factors(i)
+            load_operands(i - 1)
+
         identity = const.tile([P, P], F32, name="identity")
         make_identity(nc, identity[:])
         tau30 = const.tile([P, PACK], F32, name="tau30")
@@ -133,54 +150,89 @@ def tile_liquidcell_pa_t_v_kernel(
             for half in range(2):
                 acc[(m, half)] = psum.tile([P, WIDTH], F32, name="acc_%d_%d" % (m, half))
 
-        def multiply(i):
+        def multiply(i, half, operand):
             dl_codes, dl_scales = packed[(i, "dl")]
+            codes, scales = packed[(i, operand)]
             for m in range(M_TILES):
                 rows = slice(m * P, (m + 1) * P)
-                for half, operand in enumerate(("x", "h")):
-                    codes, scales = packed[(i, operand)]
-                    nc.tensor.matmul_mx(
-                        out=acc[(m, half)][:],
-                        lhsT=dl_codes[:, rows].bitcast(E5M2_X4),
-                        lhsT_scale=dl_scales[:, rows],
-                        rhs=codes[:].bitcast(E4M3_X4),
-                        rhs_scale=scales[:],
-                        start=(i == 0),
-                        stop=(i == CHUNKS - 1),
-                    )
+                nc.tensor.matmul_mx(
+                    out=acc[(m, half)][:],
+                    lhsT=dl_codes[:, rows].bitcast(E5M2_X4),
+                    lhsT_scale=dl_scales[:, rows],
+                    rhs=codes[:].bitcast(E4M3_X4),
+                    rhs_scale=scales[:],
+                    start=(i == 0),
+                    stop=(i == CHUNKS - 1),
+                )
 
-        for i in range(CHUNKS):
-            logit = raw[i]["logit"][:].rearrange("p t w -> p (t w)")
-            product = raw[i]["product"][:].rearrange("p t w -> p (t w)")
-            grad = raw[i]["grad"][:].rearrange("p t w -> p (t w)")
-            copy = nc.vector.tensor_copy if i < VECTOR_REGROUP_CHUNKS else nc.scalar.copy
-
+        def sigmoid_factor(i, tokens):
+            logit = raw[(i, "logit")][:, tokens, :]
             nc.scalar.activation(out=logit, in_=logit, func=ACT.Tanh, bias=HALF_LN3, scale=0.5)
-            regroup(copy, i, "x")
             nc.scalar.activation(out=logit, in_=logit, func=ACT.Square)
-            regroup(copy, i, "h")
 
-            nc.vector.tensor_tensor(out=product, in0=grad, in1=product, op=ALU.mult)
-            if i > 0:
-                quantise(i - 1, "dl", E5M2_X4)
-                multiply(i - 1)
-            quantise(i, "x", E4M3_X4)
+        def first_product(i, tokens):
+            product = raw[(i, "product")][:, tokens, :]
+            nc.vector.tensor_tensor(out=product, in0=raw[(i, "grad")][:, tokens, :], in1=product, op=ALU.mult)
+
+        def second_product(i, tokens):
+            product = raw[(i, "product")][:, tokens, :]
             nc.vector.scalar_tensor_tensor(
-                out=product, in0=logit, scalar=1.0, in1=product, op0=ALU.subtract, op1=ALU.mult
+                out=product,
+                in0=raw[(i, "logit")][:, tokens, :],
+                scalar=1.0,
+                in1=product,
+                op0=ALU.subtract,
+                op1=ALU.mult,
             )
-            quantise(i, "h", E4M3_X4)
+
+        def third_product(i):
             dl_ready = grouped.tile([P, WIDTH, PACK], BF16, name="ready_dl", align_bytes=64)
             nc.vector.tensor_tensor(
-                out=by_column(dl_ready[:]), in0=by_token(raw[i]["product"][:]), in1=gain_by_token, op=ALU.mult
+                out=by_column(dl_ready[:]), in0=by_token(raw[(i, "product")][:]), in1=gain_by_token, op=ALU.mult
             )
             ready[(i, "dl")] = dl_ready
-            if i + LOAD_BUFS < CHUNKS:
-                load(i + LOAD_BUFS)
-        quantise(CHUNKS - 1, "dl", E5M2_X4)
-        multiply(CHUNKS - 1)
 
-        for m in range(M_TILES):
-            result = results.tile([P, 2 * WIDTH], F32, name="result")
-            nc.scalar.copy(out=result[:, :WIDTH], in_=acc[(m, 0)][:])
-            nc.vector.tensor_copy(out=result[:, WIDTH:], in_=acc[(m, 1)][:])
-            nc.sync.dma_start(out=out[m * P : (m + 1) * P, :], in_=result[:])
+        def hidden_copy(i):
+            return nc.vector.tensor_copy if i % VECTOR_SHARE == 1 else nc.scalar.copy
+
+        def refill(i):
+            if i + LOAD_BUFS < CHUNKS:
+                load_factors(i + LOAD_BUFS)
+            if i + LOAD_BUFS - 1 < CHUNKS:
+                load_operands(i + LOAD_BUFS - 1)
+
+        for tokens in token_pieces(0):
+            sigmoid_factor(0, tokens)
+            first_product(0, tokens)
+            second_product(0, tokens)
+        third_product(0)
+        refill(0)
+        for i in range(1, CHUNKS):
+            (tokens,) = token_pieces(i)
+            sigmoid_factor(i, tokens)
+            regroup(nc.scalar.copy, i - 1, "x")
+            first_product(i, tokens)
+            regroup(hidden_copy(i - 1), i - 1, "h")
+            quantise(i - 1, "x", E4M3_X4)
+            second_product(i, tokens)
+            quantise(i - 1, "dl", E5M2_X4)
+            multiply(i - 1, 0, "x")
+            third_product(i)
+            quantise(i - 1, "h", E4M3_X4)
+            multiply(i - 1, 1, "h")
+            refill(i)
+        last = CHUNKS - 1
+        regroup(nc.scalar.copy, last, "x")
+        regroup(hidden_copy(last), last, "h")
+        quantise(last, "x", E4M3_X4)
+        quantise(last, "dl", E5M2_X4)
+        multiply(last, 0, "x")
+        quantise(last, "h", E4M3_X4)
+        multiply(last, 1, "h")
+
+        for half in range(2):
+            for m in range(M_TILES):
+                result = results.tile([P, WIDTH], F32, name="result")
+                copy = nc.scalar.copy if m % 2 == 0 else nc.vector.tensor_copy
+                copy(out=result[:], in_=acc[(m, half)][:])
+                nc.sync.dma_start(out=out[m * P : (m + 1) * P, half * WIDTH : (half + 1) * WIDTH], in_=result[:])

@@ -22,11 +22,13 @@ CHUNKS = TOKENS // K_PASS
 M_TILES = WIDTH // P
 RUN = 4
 
-LOAD_BUFS = 4
-FIRST_CHUNK_PIECES = 2
-VECTOR_SHARE = 4
-
 HALF_LN3 = 0.5 * math.log(3.0)
+TAU_FACTOR = 30.0
+
+LOAD_BUFS = 4
+STAGE_BUFS = 3
+FIRST_CHUNK_PIECES = 2
+VECTOR_HIDDEN_CHUNK = 1
 
 FLOPS = 2 * TOKENS * WIDTH * (2 * WIDTH)
 BYTES = 3 * TOKENS * WIDTH * 2 + 2 * TOKENS * WIDTH * 4 + WIDTH * 2 + WIDTH * 2 * WIDTH * 4
@@ -36,8 +38,7 @@ def chunk_rows(tensor, i):
     return tensor[i * K_PASS : (i + 1) * K_PASS, :].rearrange("(p t) w -> p t w", t=PACK)
 
 
-def token_pieces(i):
-    pieces = FIRST_CHUNK_PIECES if i == 0 else 1
+def token_pieces(pieces):
     tokens = PACK // pieces
     return [slice(k * tokens, (k + 1) * tokens) for k in range(pieces)]
 
@@ -69,8 +70,8 @@ def tile_liquidcell_pa_t_v_kernel(
     with ExitStack() as ctx:
         const = ctx.enter_context(tc.tile_pool(name="const", bufs=1))
         loads = ctx.enter_context(tc.tile_pool(name="loads", bufs=LOAD_BUFS))
-        grouped = ctx.enter_context(tc.tile_pool(name="grouped", bufs=3))
-        quant = ctx.enter_context(tc.tile_pool(name="quant", bufs=3))
+        grouped = ctx.enter_context(tc.tile_pool(name="grouped", bufs=STAGE_BUFS))
+        quant = ctx.enter_context(tc.tile_pool(name="quant", bufs=STAGE_BUFS))
         results = ctx.enter_context(tc.tile_pool(name="results", bufs=2 * M_TILES))
         psum = ctx.enter_context(tc.psum_pool(name="psum", bufs=1))
         ctx.enter_context(tc.manual_schedule())
@@ -83,7 +84,7 @@ def tile_liquidcell_pa_t_v_kernel(
             logit = loads.tile([P, PACK, WIDTH], F32, name="logit")
             grad = loads.tile([P, PACK, WIDTH], BF16, name="grad")
             product = loads.tile([P, PACK, WIDTH], F32, name="product")
-            for tokens in token_pieces(i):
+            for tokens in token_pieces(FIRST_CHUNK_PIECES if i == 0 else 1):
                 nc.sync.dma_start(out=logit[:, tokens, :], in_=chunk_rows(tau_logits, i)[:, tokens, :])
                 nc.sync.dma_start(out=grad[:, tokens, :], in_=chunk_rows(grad_out, i)[:, tokens, :])
                 nc.sync.dma_start(out=product[:, tokens, :], in_=chunk_rows(drive, i)[:, tokens, :])
@@ -99,35 +100,27 @@ def tile_liquidcell_pa_t_v_kernel(
             raw[(i, "x")] = x_raw
             raw[(i, "h")] = h_raw
 
-        def regroup(copy, i, operand):
-            tile = grouped.tile([P, WIDTH, PACK], BF16, name="ready_" + operand, align_bytes=64)
-            copy(out=by_column(tile[:]), in_=by_token(raw[(i, operand)][:]))
-            ready[(i, operand)] = tile
-
-        def quantise(i, operand, fmt):
-            codes = quant.tile([P, WIDTH], U32, name="codes_" + operand, align_bytes=64)
-            scales = quant.tile([P, WIDTH], U8, name="scales_" + operand, align_bytes=64)
-            nc.vector.quantize_mx(
-                out=codes[:].bitcast(fmt),
-                scales=scales[:],
-                in_=ready[(i, operand)][:].rearrange("p w t -> p (w t)"),
-            )
-            packed[(i, operand)] = (codes, scales)
-
-        tau_col = const.tile([P, PACK], BF16, name="tau_col")
-        nc.sync.dma_start(out=tau_col[:], in_=tau_base.rearrange("(p a) -> p a", a=PACK))
         load_factors(0)
         for i in range(1, LOAD_BUFS):
             load_factors(i)
             load_operands(i - 1)
 
+        def refill(i):
+            if i + LOAD_BUFS < CHUNKS:
+                load_factors(i + LOAD_BUFS)
+            if i + LOAD_BUFS - 1 < CHUNKS:
+                load_operands(i + LOAD_BUFS - 1)
+
+        tau_col = const.tile([P, PACK], BF16, name="tau_col")
+        nc.scalar.dma_start(out=tau_col[:], in_=tau_base.rearrange("(p a) -> p a", a=PACK))
         identity = const.tile([P, P], F32, name="identity")
         make_identity(nc, identity[:])
-        tau30 = const.tile([P, PACK], F32, name="tau30")
-        nc.vector.tensor_scalar(out=tau30[:], in0=tau_col[:], scalar1=30.0, scalar2=None, op0=ALU.mult)
+        tau_scaled = const.tile([P, PACK], F32, name="tau_scaled")
+        nc.vector.tensor_scalar(out=tau_scaled[:], in0=tau_col[:], scalar1=TAU_FACTOR, scalar2=None, op0=ALU.mult)
         gain_col = const.tile([P, PACK], F32, name="gain_col")
-        nc.vector.reciprocal(out=gain_col[:], in_=tau30[:])
-        gain_psum = psum.tile([P, PACK, P], F32, name="gain_psum", tag="acc_3_1")
+        nc.vector.reciprocal(out=gain_col[:], in_=tau_scaled[:])
+        last_bank = "acc_%d_%d" % (M_TILES - 1, 1)
+        gain_psum = psum.tile([P, PACK, P], F32, name="gain_psum", tag=last_bank)
         for a in range(PACK):
             nc.tensor.matmul(
                 out=gain_psum[:, a, :],
@@ -150,25 +143,13 @@ def tile_liquidcell_pa_t_v_kernel(
             for half in range(2):
                 acc[(m, half)] = psum.tile([P, WIDTH], F32, name="acc_%d_%d" % (m, half))
 
-        def multiply(i, half, operand):
-            dl_codes, dl_scales = packed[(i, "dl")]
-            codes, scales = packed[(i, operand)]
-            for m in range(M_TILES):
-                rows = slice(m * P, (m + 1) * P)
-                nc.tensor.matmul_mx(
-                    out=acc[(m, half)][:],
-                    lhsT=dl_codes[:, rows].bitcast(E5M2_X4),
-                    lhsT_scale=dl_scales[:, rows],
-                    rhs=codes[:].bitcast(E4M3_X4),
-                    rhs_scale=scales[:],
-                    start=(i == 0),
-                    stop=(i == CHUNKS - 1),
-                )
-
-        def sigmoid_factor(i, tokens):
-            logit = raw[(i, "logit")][:, tokens, :]
-            nc.scalar.activation(out=logit, in_=logit, func=ACT.Tanh, bias=HALF_LN3, scale=0.5)
-            nc.scalar.activation(out=logit, in_=logit, func=ACT.Square)
+        def sigmoid_factor(i, pieces):
+            for tokens in pieces:
+                logit = raw[(i, "logit")][:, tokens, :]
+                nc.scalar.activation(out=logit, in_=logit, func=ACT.Tanh, bias=HALF_LN3, scale=0.5)
+            for tokens in pieces:
+                logit = raw[(i, "logit")][:, tokens, :]
+                nc.scalar.activation(out=logit, in_=logit, func=ACT.Square)
 
         def first_product(i, tokens):
             product = raw[(i, "product")][:, tokens, :]
@@ -192,35 +173,61 @@ def tile_liquidcell_pa_t_v_kernel(
             )
             ready[(i, "dl")] = dl_ready
 
+        def regroup(copy, i, operand):
+            tile = grouped.tile([P, WIDTH, PACK], BF16, name="ready_" + operand, align_bytes=64)
+            copy(out=by_column(tile[:]), in_=by_token(raw[(i, operand)][:]))
+            ready[(i, operand)] = tile
+
         def hidden_copy(i):
-            return nc.vector.tensor_copy if i % VECTOR_SHARE == 1 else nc.scalar.copy
+            return nc.vector.tensor_copy if i == VECTOR_HIDDEN_CHUNK else nc.scalar.copy
 
-        def refill(i):
-            if i + LOAD_BUFS < CHUNKS:
-                load_factors(i + LOAD_BUFS)
-            if i + LOAD_BUFS - 1 < CHUNKS:
-                load_operands(i + LOAD_BUFS - 1)
+        def quantise(i, operand, fmt):
+            codes = quant.tile([P, WIDTH], U32, name="codes_" + operand, align_bytes=64)
+            scales = quant.tile([P, WIDTH], U8, name="scales_" + operand, align_bytes=64)
+            nc.vector.quantize_mx(
+                out=codes[:].bitcast(fmt),
+                scales=scales[:],
+                in_=ready[(i, operand)][:].rearrange("p w t -> p (w t)"),
+            )
+            packed[(i, operand)] = (codes, scales)
 
-        for tokens in token_pieces(0):
-            sigmoid_factor(0, tokens)
+        def multiply(i, half, operand):
+            dl_codes, dl_scales = packed[(i, "dl")]
+            codes, scales = packed[(i, operand)]
+            for m in range(M_TILES):
+                rows = slice(m * P, (m + 1) * P)
+                nc.tensor.matmul_mx(
+                    out=acc[(m, half)][:],
+                    lhsT=dl_codes[:, rows].bitcast(E5M2_X4),
+                    lhsT_scale=dl_scales[:, rows],
+                    rhs=codes[:].bitcast(E4M3_X4),
+                    rhs_scale=scales[:],
+                    start=(i == 0),
+                    stop=(i == CHUNKS - 1),
+                )
+
+        for tokens in token_pieces(FIRST_CHUNK_PIECES):
+            sigmoid_factor(0, [tokens])
             first_product(0, tokens)
             second_product(0, tokens)
         third_product(0)
         refill(0)
+
+        (all_tokens,) = token_pieces(1)
         for i in range(1, CHUNKS):
-            (tokens,) = token_pieces(i)
-            sigmoid_factor(i, tokens)
+            sigmoid_factor(i, token_pieces(2))
             regroup(nc.scalar.copy, i - 1, "x")
-            first_product(i, tokens)
+            first_product(i, all_tokens)
             regroup(hidden_copy(i - 1), i - 1, "h")
-            quantise(i - 1, "x", E4M3_X4)
-            second_product(i, tokens)
             quantise(i - 1, "dl", E5M2_X4)
+            second_product(i, all_tokens)
+            quantise(i - 1, "x", E4M3_X4)
             multiply(i - 1, 0, "x")
-            third_product(i)
             quantise(i - 1, "h", E4M3_X4)
             multiply(i - 1, 1, "h")
+            third_product(i)
             refill(i)
+
         last = CHUNKS - 1
         regroup(nc.scalar.copy, last, "x")
         regroup(hidden_copy(last), last, "h")

import math
from contextlib import ExitStack

import concourse.mybir as mybir
from concourse.masks import make_identity

F32 = mybir.dt.float32
BF16 = mybir.dt.bfloat16
U32 = mybir.dt.uint32
U8 = mybir.dt.uint8
E4M3_X4 = mybir.dt.float8_e4m3fn_x4
E5M2_X4 = mybir.dt.float8_e5m2_x4
ACT = mybir.ActivationFunctionType
ALU = mybir.AluOpType

P = 128
PACK = 4
K_PASS = P * PACK
TOKENS = 4096
WIDTH = 512
CHUNKS = TOKENS // K_PASS
M_TILES = WIDTH // P
RUN = 4

HALF_LN3 = 0.5 * math.log(3.0)
TAU_FACTOR = 30.0

LOAD_BUFS = 4
STAGE_BUFS = 3
FIRST_CHUNK_PIECES = 2
VECTOR_HIDDEN_CHUNK = 1

FLOPS = 2 * TOKENS * WIDTH * (2 * WIDTH)
BYTES = 3 * TOKENS * WIDTH * 2 + 2 * TOKENS * WIDTH * 4 + WIDTH * 2 + WIDTH * 2 * WIDTH * 4


def chunk_rows(tensor, i):
    return tensor[i * K_PASS : (i + 1) * K_PASS, :].rearrange("(p t) w -> p t w", t=PACK)


def token_pieces(pieces):
    tokens = PACK // pieces
    return [slice(k * tokens, (k + 1) * tokens) for k in range(pieces)]


def by_token(tile_ap):
    return tile_ap.rearrange("p t (c i) -> p c t i", i=RUN)


def by_column(tile_ap):
    return tile_ap.rearrange("p (c i) t -> p c t i", i=RUN)


def tile_liquidcell_pa_t_v_kernel(
    tc,
    x,
    hidden,
    W_rec,
    W_in_w,
    W_in_b,
    tau_base,
    tau_adapt_w,
    tau_adapt_b,
    tau_logits,
    drive,
    grad_out,
    out,
):
    nc = tc.nc
    with ExitStack() as ctx:
        const = ctx.enter_context(tc.tile_pool(name="const", bufs=1))
        loads = ctx.enter_context(tc.tile_pool(name="loads", bufs=LOAD_BUFS))
        grouped = ctx.enter_context(tc.tile_pool(name="grouped", bufs=STAGE_BUFS))
        quant = ctx.enter_context(tc.tile_pool(name="quant", bufs=STAGE_BUFS))
        results = ctx.enter_context(tc.tile_pool(name="results", bufs=2 * M_TILES))
        psum = ctx.enter_context(tc.psum_pool(name="psum", bufs=1))
        ctx.enter_context(tc.manual_schedule())

        raw = {}
        ready = {}
        packed = {}

        def load_factors(i):
            logit = loads.tile([P, PACK, WIDTH], F32, name="logit")
            grad = loads.tile([P, PACK, WIDTH], BF16, name="grad")
            product = loads.tile([P, PACK, WIDTH], F32, name="product")
            for tokens in token_pieces(FIRST_CHUNK_PIECES if i == 0 else 1):
                nc.sync.dma_start(out=logit[:, tokens, :], in_=chunk_rows(tau_logits, i)[:, tokens, :])
                nc.sync.dma_start(out=grad[:, tokens, :], in_=chunk_rows(grad_out, i)[:, tokens, :])
                nc.sync.dma_start(out=product[:, tokens, :], in_=chunk_rows(drive, i)[:, tokens, :])
            raw[(i, "logit")] = logit
            raw[(i, "grad")] = grad
            raw[(i, "product")] = product

        def load_operands(i):
            x_raw = loads.tile([P, PACK, WIDTH], BF16, name="x_raw")
            nc.sync.dma_start(out=x_raw[:], in_=chunk_rows(x, i))
            h_raw = loads.tile([P, PACK, WIDTH], BF16, name="h_raw")
            nc.sync.dma_start(out=h_raw[:], in_=chunk_rows(hidden, i))
            raw[(i, "x")] = x_raw
            raw[(i, "h")] = h_raw

        load_factors(0)
        for i in range(1, LOAD_BUFS):
            load_factors(i)
            load_operands(i - 1)

        def refill(i):
            if i + LOAD_BUFS < CHUNKS:
                load_factors(i + LOAD_BUFS)
            if i + LOAD_BUFS - 1 < CHUNKS:
                load_operands(i + LOAD_BUFS - 1)

        tau_col = const.tile([P, PACK], BF16, name="tau_col")
        nc.scalar.dma_start(out=tau_col[:], in_=tau_base.rearrange("(p a) -> p a", a=PACK))
        identity = const.tile([P, P], F32, name="identity")
        make_identity(nc, identity[:])
        tau_scaled = const.tile([P, PACK], F32, name="tau_scaled")
        nc.vector.tensor_scalar(out=tau_scaled[:], in0=tau_col[:], scalar1=TAU_FACTOR, scalar2=None, op0=ALU.mult)
        gain_col = const.tile([P, PACK], F32, name="gain_col")
        nc.vector.reciprocal(out=gain_col[:], in_=tau_scaled[:])
        last_bank = "acc_%d_%d" % (M_TILES - 1, 1)
        gain_psum = psum.tile([P, PACK, P], F32, name="gain_psum", tag=last_bank)
        for a in range(PACK):
            nc.tensor.matmul(
                out=gain_psum[:, a, :],
                lhsT=gain_col[:, a : a + 1].to_broadcast([P, P]),
                rhs=identity[:],
                start=True,
                stop=True,
            )
        gain = const.tile([P, WIDTH], F32, name="gain")
        nc.vector.tensor_copy(
            out=gain[:].rearrange("p (n a) -> p n a", a=PACK),
            in_=gain_psum[:].rearrange("p a n -> p n a"),
        )
        gain_by_token = (
            gain[:].rearrange("p (c i) -> p c i", i=RUN).unsqueeze(2).to_broadcast([P, WIDTH // RUN, PACK, RUN])
        )

        acc = {}
        for m in range(M_TILES):
            for half in range(2):
                acc[(m, half)] = psum.tile([P, WIDTH], F32, name="acc_%d_%d" % (m, half))

        def sigmoid_factor(i, pieces):
            for tokens in pieces:
                logit = raw[(i, "logit")][:, tokens, :]
                nc.scalar.activation(out=logit, in_=logit, func=ACT.Tanh, bias=HALF_LN3, scale=0.5)
            for tokens in pieces:
                logit = raw[(i, "logit")][:, tokens, :]
                nc.scalar.activation(out=logit, in_=logit, func=ACT.Square)

        def first_product(i, tokens):
            product = raw[(i, "product")][:, tokens, :]
            nc.vector.tensor_tensor(out=product, in0=raw[(i, "grad")][:, tokens, :], in1=product, op=ALU.mult)

        def second_product(i, tokens):
            product = raw[(i, "product")][:, tokens, :]
            nc.vector.scalar_tensor_tensor(
                out=product,
                in0=raw[(i, "logit")][:, tokens, :],
                scalar=1.0,
                in1=product,
                op0=ALU.subtract,
                op1=ALU.mult,
            )

        def third_product(i):
            dl_ready = grouped.tile([P, WIDTH, PACK], BF16, name="ready_dl", align_bytes=64)
            nc.vector.tensor_tensor(
                out=by_column(dl_ready[:]), in0=by_token(raw[(i, "product")][:]), in1=gain_by_token, op=ALU.mult
            )
            ready[(i, "dl")] = dl_ready

        def regroup(copy, i, operand):
            tile = grouped.tile([P, WIDTH, PACK], BF16, name="ready_" + operand, align_bytes=64)
            copy(out=by_column(tile[:]), in_=by_token(raw[(i, operand)][:]))
            ready[(i, operand)] = tile

        def hidden_copy(i):
            return nc.vector.tensor_copy if i == VECTOR_HIDDEN_CHUNK else nc.scalar.copy

        def quantise(i, operand, fmt):
            codes = quant.tile([P, WIDTH], U32, name="codes_" + operand, align_bytes=64)
            scales = quant.tile([P, WIDTH], U8, name="scales_" + operand, align_bytes=64)
            nc.vector.quantize_mx(
                out=codes[:].bitcast(fmt),
                scales=scales[:],
                in_=ready[(i, operand)][:].rearrange("p w t -> p (w t)"),
            )
            packed[(i, operand)] = (codes, scales)

        def multiply(i, half, operand):
            dl_codes, dl_scales = packed[(i, "dl")]
            codes, scales = packed[(i, operand)]
            for m in range(M_TILES):
                rows = slice(m * P, (m + 1) * P)
                nc.tensor.matmul_mx(
                    out=acc[(m, half)][:],
                    lhsT=dl_codes[:, rows].bitcast(E5M2_X4),
                    lhsT_scale=dl_scales[:, rows],
                    rhs=codes[:].bitcast(E4M3_X4),
                    rhs_scale=scales[:],
                    start=(i == 0),
                    stop=(i == CHUNKS - 1),
                )

        for tokens in token_pieces(FIRST_CHUNK_PIECES):
            sigmoid_factor(0, [tokens])
            first_product(0, tokens)
            second_product(0, tokens)
        third_product(0)
        refill(0)

        (all_tokens,) = token_pieces(1)
        for i in range(1, CHUNKS):
            sigmoid_factor(i, token_pieces(2))
            regroup(nc.scalar.copy, i - 1, "x")
            first_product(i, all_tokens)
            regroup(hidden_copy(i - 1), i - 1, "h")
            quantise(i - 1, "dl", E5M2_X4)
            second_product(i, all_tokens)
            quantise(i - 1, "x", E4M3_X4)
            multiply(i - 1, 0, "x")
            quantise(i - 1, "h", E4M3_X4)
            multiply(i - 1, 1, "h")
            third_product(i)
            refill(i)

        last = CHUNKS - 1
        regroup(nc.scalar.copy, last, "x")
        regroup(hidden_copy(last), last, "h")
        quantise(last, "x", E4M3_X4)
        quantise(last, "dl", E5M2_X4)
        multiply(last, 0, "x")
        quantise(last, "h", E4M3_X4)
        multiply(last, 1, "h")

        for half in range(2):
            for m in range(M_TILES):
                result = results.tile([P, WIDTH], F32, name="result")
                copy = nc.scalar.copy if m % 2 == 0 else nc.vector.tensor_copy
                copy(out=result[:], in_=acc[(m, half)][:])
                nc.sync.dma_start(out=out[m * P : (m + 1) * P, half * WIDTH : (half + 1) * WIDTH], in_=result[:])
